import numpy as np
import ml_dtypes


def mxq(x, axis, fmt="e4m3"):
    dtype, down = {"e4m3": (ml_dtypes.float8_e4m3fn, 7), "e5m2": (ml_dtypes.float8_e5m2, 14)}[fmt]
    v = np.moveaxis(np.asarray(x, np.float32).astype(ml_dtypes.bfloat16).astype(np.float64), axis, -1)
    blocks = v.reshape(v.shape[:-1] + (-1, 32))
    amax = np.abs(blocks).max(-1, keepdims=True)
    byte = np.maximum(np.where(amax > 0, np.frexp(amax)[1] - 1 + 127, 0) - down, 1)
    scale = np.exp2(byte - 127.0)
    codes = (blocks / scale).astype(np.float32).astype(dtype).astype(np.float64)
    return np.moveaxis((codes * scale).reshape(v.shape), -1, axis)


WIDE = False


def mx_kscale(k):
    if not WIDE:
        return np.ones(k)
    levels = np.array([10, -10, 5, -5, 0])
    a = np.random.permutation(np.resize(levels, k // 512 * 4)).reshape(k // 512, 4)
    idx = np.arange(k)
    return np.exp2(a[idx // 512, idx % 128 // 32])


BF16 = ml_dtypes.bfloat16


def bf(x):
    return np.asarray(x, np.float32).astype(BF16)


def f64(x):
    return np.asarray(x).astype(np.float64)


B, S, D, H = 4, 1024, 256, 2
LN_EPS = 1e-5
SIGMA = 1.96


def layer_norm(v, gamma, beta):
    mu = v.mean(-1, keepdims=True)
    var = v.var(-1, keepdims=True)
    return (v - mu) * (1.0 / np.sqrt(var + LN_EPS)) * gamma + beta


def setup_inputs():
    s = mx_kscale(S)
    z = np.random.standard_normal((B, H, S, S)) * SIGMA
    e = np.exp(z - z.max(-1, keepdims=True))
    return {"probs": bf(e / e.sum(-1, keepdims=True) * s),
            "x": bf(np.random.standard_normal((B, S, D)) / s[:, None]),
            "Wv": bf(np.random.standard_normal((H * D, D)) * 0.25 * np.sqrt(S / (H * D))),
            "gamma": bf(1.0 + 0.1 * np.random.standard_normal(D)),
            "beta": bf(0.1 * np.random.standard_normal(D))}


def reference(probs, x, Wv, gamma, beta):
    xf = f64(x)
    ctx = mxq(f64(probs), 3, "e4m3") @ mxq(xf, 1, "e4m3")[:, None]
    merged = ctx.transpose(0, 2, 1, 3).reshape(B, S, H * D)
    y = (mxq(merged, 2, "e4m3") @ mxq(f64(Wv), 0, "e4m3")) + xf
    return layer_norm(y, f64(gamma), f64(beta))

@@ -1,0 +1,316 @@
+from contextlib import ExitStack
+
+import concourse.mybir as mybir
+from concourse.masks import make_identity
+
+F32 = mybir.dt.float32
+BF16 = mybir.dt.bfloat16
+U32 = mybir.dt.uint32
+U8 = mybir.dt.uint8
+FP8X4 = mybir.dt.float8_e4m3fn_x4
+ALU = mybir.AluOpType
+ACT = mybir.ActivationFunctionType
+
+B, H, S, D = 4, 2, 1024, 256
+LN_EPS = 1e-5
+FLOPS = 2 * B * H * S * S * D + 2 * B * S * (H * D) * D
+
+P = 128
+PACK = 4
+PASSES = S // (P * PACK)
+TURNS = 2
+ROW_PAIR = 2
+SLAB = P * ROW_PAIR
+SLABS = S // SLAB
+N_SLABS = B * SLABS
+HALVES = D // P
+HEAD_WORDS = PASSES * SLAB
+AHEAD = 4
+assert AHEAD >= B
+
+
+def tile_bertselfattention_pb_t_kernel(tc, probs, x, Wv, gamma, beta, out):
+    nc = tc.nc
+    with ExitStack() as stack:
+        consts = stack.enter_context(tc.tile_pool(name="consts", bufs=1))
+        rows_pool = stack.enter_context(tc.tile_pool(name="rows", bufs=AHEAD + 1))
+        x_pool = stack.enter_context(tc.tile_pool(name="x", bufs=2))
+        work = stack.enter_context(tc.tile_pool(name="work", bufs=2))
+        norm = stack.enter_context(tc.tile_pool(name="norm", bufs=3))
+        turn_banks = stack.enter_context(tc.psum_pool(name="turn_banks", bufs=4))
+        ctx_banks = stack.enter_context(tc.psum_pool(name="ctx_banks", bufs=2))
+        y_banks = stack.enter_context(tc.psum_pool(name="y_banks", bufs=2))
+        stack.enter_context(tc.manual_schedule())
+
+        rows_of, grouped_of, codes_of, scales_of = {}, {}, {}, {}
+        merged_of, m_codes_of, m_scales_of, y_of = {}, {}, {}, {}
+        yres_of, neg_mean_of, std_of, scaled_of = {}, {}, {}, {}
+        x_rows_of, x_grouped_of, x_codes_of, x_scales_of = {}, {}, {}, {}
+
+        def load_slab(n):
+            b, a = divmod(n, SLABS)
+            rows = rows_pool.tile([P, H * ROW_PAIR * S], BF16)
+            for h in range(H):
+                nc.sync.dma_start(
+                    out=rows[:, h * ROW_PAIR * S : (h + 1) * ROW_PAIR * S],
+                    in_=probs[b, h, a * SLAB : (a + 1) * SLAB, :].rearrange(
+                        "(p r) j -> p (r j)", r=ROW_PAIR
+                    ),
+                )
+            rows_of[n] = rows
+
+        def load_x(b):
+            x_rows = x_pool.tile([P, SLABS * ROW_PAIR, D], BF16, bufs=B)
+            nc.sync.dma_start(
+                out=x_rows[:].rearrange("p (a r) d -> p a (r d)", r=ROW_PAIR),
+                in_=x[b].rearrange("(a p r) d -> p a (r d)", p=P, r=ROW_PAIR),
+            )
+            x_rows_of[b] = x_rows
+
+        def regroup(grouped, planes):
+            nc.vector.tensor_copy(
+                out=grouped.rearrange("p (c i) t -> p c t i", i=4),
+                in_=planes.rearrange("p t (c i) -> p c t i", i=4),
+            )
+
+        def regroup_x(b):
+            x_grouped = x_pool.tile([P, PASSES, D, PACK], BF16, align_bytes=64)
+            for g in range(PASSES):
+                regroup(x_grouped[:, g, :, :], x_rows_of[b][:, g * PACK : (g + 1) * PACK, :])
+            x_grouped_of[b] = x_grouped
+
+        def quantise_x(b):
+            x_codes = x_pool.tile([P, PASSES * D], U32, align_bytes=64)
+            x_scales = x_pool.tile([P, PASSES * D], U8, align_bytes=64)
+            nc.vector.quantize_mx(
+                out=x_codes[:].bitcast(FP8X4),
+                scales=x_scales[:],
+                in_=x_grouped_of[b][:].rearrange("p g d t -> p (g d t)"),
+            )
+            x_codes_of[b], x_scales_of[b] = x_codes, x_scales
+
+        def turn_head(n, h):
+            if h == 0:
+                grouped = work.tile([P, H * HEAD_WORDS * PACK], BF16, align_bytes=64)
+                grouped_of[n] = grouped
+            words = rows_of[n][:].bitcast(F32).rearrange(
+                "p (h r w) -> p h r w", h=H, r=ROW_PAIR
+            )
+            grouped_words = grouped_of[n][:].bitcast(F32).rearrange(
+                "p (h g c u) -> p h g c u", h=H, g=PASSES, u=TURNS
+            )
+            for g in range(PASSES):
+                turned = turn_banks.tile([P, TURNS, SLAB], F32)
+                for u in range(TURNS):
+                    first = (g * TURNS + u) * P
+                    for r in range(ROW_PAIR):
+                        nc.tensor.transpose(
+                            turned[:, u, r * P : (r + 1) * P],
+                            words[:, h, r, first : first + P],
+                            ident[:],
+                        )
+                nc.scalar.copy(
+                    out=grouped_words[:, h, g, :, :], in_=turned[:].rearrange("p u c -> p c u")
+                )
+
+        def quantise_head(n, h):
+            if h == 0:
+                codes = work.tile([P, H * HEAD_WORDS], U32, align_bytes=64)
+                scales = work.tile([P, H * HEAD_WORDS], U8, align_bytes=64)
+                codes_of[n], scales_of[n] = codes, scales
+            cols = slice(h * HEAD_WORDS, (h + 1) * HEAD_WORDS)
+            nc.vector.quantize_mx(
+                out=codes_of[n][:, cols].bitcast(FP8X4),
+                scales=scales_of[n][:, cols],
+                in_=grouped_of[n][:, h * HEAD_WORDS * PACK : (h + 1) * HEAD_WORDS * PACK],
+            )
+
+        def pool_values(n):
+            b = n // SLABS
+            merged = work.tile([P, ROW_PAIR, P, PACK], BF16, align_bytes=64)
+            for r in range(ROW_PAIR):
+                ctx_t = ctx_banks.tile([P, PACK, P], F32)
+                for h in range(H):
+                    for half in range(HALVES):
+                        for g in range(PASSES):
+                            x_cols = slice(g * D + half * P, g * D + (half + 1) * P)
+                            first = h * HEAD_WORDS + g * SLAB + r * P
+                            nc.tensor.matmul_mx(
+                                out=ctx_t[:, h * HALVES + half, :],
+                                lhsT=x_codes_of[b][:, x_cols].bitcast(FP8X4),
+                                lhsT_scale=x_scales_of[b][:, x_cols],
+                                rhs=codes_of[n][:, first : first + P].bitcast(FP8X4),
+                                rhs_scale=scales_of[n][:, first : first + P],
+                                start=(g == 0),
+                                stop=(g == PASSES - 1),
+                            )
+                nc.scalar.copy(out=merged[:, r, :, :], in_=ctx_t[:].rearrange("p t i -> p i t"))
+            merged_of[n] = merged
+
+        def quantise_merged(n):
+            m_codes = work.tile([P, SLAB], U32, align_bytes=64)
+            m_scales = work.tile([P, SLAB], U8, align_bytes=64)
+            nc.vector.quantize_mx(
+                out=m_codes[:].bitcast(FP8X4),
+                scales=m_scales[:],
+                in_=merged_of[n][:].rearrange("p r i t -> p (r i t)"),
+            )
+            m_codes_of[n], m_scales_of[n] = m_codes, m_scales
+
+        def project(n):
+            y = y_banks.tile([P, ROW_PAIR, D], F32)
+            for r in range(ROW_PAIR):
+                nc.tensor.matmul_mx(
+                    out=y[:, r, :],
+                    lhsT=m_codes_of[n][:, r * P : (r + 1) * P].bitcast(FP8X4),
+                    lhsT_scale=m_scales_of[n][:, r * P : (r + 1) * P],
+                    rhs=w_codes[:].bitcast(FP8X4),
+                    rhs_scale=w_scales[:],
+                    start=True,
+                    stop=True,
+                )
+            y_of[n] = y
+
+        def add_residual(n):
+            b, a = divmod(n, SLABS)
+            yres = norm.tile([P, ROW_PAIR, D], F32)
+            row_sum = norm.tile([P, ROW_PAIR], F32)
+            neg_mean = norm.tile([P, ROW_PAIR], F32)
+            scaled = norm.tile([P, ROW_PAIR, D], F32)
+            for r in range(ROW_PAIR):
+                nc.vector.scalar_tensor_tensor(
+                    out=yres[:, r, :],
+                    in0=y_of[n][:, r, :],
+                    scalar=1.0,
+                    in1=x_rows_of[b][:, a * ROW_PAIR + r, :],
+                    op0=ALU.mult,
+                    op1=ALU.add,
+                    accum_out=row_sum[:, r : r + 1],
+                )
+            nc.vector.tensor_scalar(
+                out=neg_mean[:], in0=row_sum[:], scalar1=-1.0 / D, scalar2=None, op0=ALU.mult
+            )
+            for r in range(ROW_PAIR):
+                nc.vector.scalar_tensor_tensor(
+                    out=scaled[:, r, :],
+                    in0=yres[:, r, :],
+                    scalar=neg_mean[:, r : r + 1],
+                    in1=gain_bias[:, 0, :],
+                    op0=ALU.add,
+                    op1=ALU.mult,
+                )
+            yres_of[n], neg_mean_of[n], scaled_of[n] = yres, neg_mean, scaled
+
+        def deviation(n):
+            sq_sum = norm.tile([P, ROW_PAIR], F32)
+            std = norm.tile([P, ROW_PAIR], F32)
+            for r in range(ROW_PAIR):
+                squares = norm.tile([P, D], BF16)
+                nc.scalar.activation(
+                    out=squares[:],
+                    in_=yres_of[n][:, r, :],
+                    func=ACT.Square,
+                    bias=neg_mean_of[n][:, r : r + 1],
+                    scale=1.0,
+                    accum_out=sq_sum[:, r : r + 1],
+                )
+            nc.scalar.activation(
+                out=std[:], in_=sq_sum[:], func=ACT.Sqrt, bias=eps[:], scale=1.0 / D
+            )
+            std_of[n] = std
+
+        def finish(n):
+            b, a = divmod(n, SLABS)
+            rstd = norm.tile([P, ROW_PAIR], F32)
+            result = norm.tile([P, ROW_PAIR, D], F32)
+            nc.vector.reciprocal(out=rstd[:], in_=std_of[n][:])
+            for r in range(ROW_PAIR):
+                nc.vector.scalar_tensor_tensor(
+                    out=result[:, r, :],
+                    in0=scaled_of[n][:, r, :],
+                    scalar=rstd[:, r : r + 1],
+                    in1=gain_bias[:, 1, :],
+                    op0=ALU.mult,
+                    op1=ALU.add,
+                )
+            nc.sync.dma_start(
+                out=out[b, a * SLAB : (a + 1) * SLAB, :].rearrange(
+                    "(p r) e -> p r e", r=ROW_PAIR
+                ),
+                in_=result[:],
+            )
+
+        def live(n):
+            return 0 <= n < N_SLABS
+
+        ident = consts.tile([P, P], F32)
+        make_identity(nc, ident[:])
+        eps = consts.tile([P, 1], F32)
+        nc.vector.memset(eps[:], LN_EPS)
+        first_table = consts.tile([P, 1], F32)
+        nc.scalar.activation(out=first_table[:], in_=eps[:], func=ACT.Sqrt)
+
+        ones = consts.tile([P, P], BF16)
+        nc.vector.memset(ones[:], 1.0)
+        gb_row = consts.tile([P, 2, D], BF16)
+        nc.vector.memset(gb_row[:], 0.0)
+        nc.scalar.dma_start(out=gb_row[0:1, 0, :], in_=gamma.rearrange("(o e) -> o e", o=1))
+        nc.scalar.dma_start(out=gb_row[0:1, 1, :], in_=beta.rearrange("(o e) -> o e", o=1))
+        gb_bank = y_banks.tile([P, 2, D], F32, tag="y")
+        nc.tensor.matmul(
+            out=gb_bank[:].rearrange("p k e -> p (k e)"),
+            lhsT=ones[:],
+            rhs=gb_row[:].rearrange("p k e -> p (k e)"),
+            start=True,
+            stop=True,
+        )
+        gain_bias = consts.tile([P, 2, D], F32)
+        nc.scalar.copy(out=gain_bias[:], in_=gb_bank[:])
+
+        w_rows = consts.tile([P, PACK, D], BF16)
+        for n in range(AHEAD):
+            load_slab(n)
+            if n < B:
+                load_x(n)
+            if n == 0:
+                nc.sync.dma_start(out=w_rows[:], in_=Wv.rearrange("(t p) e -> p t e", p=P))
+
+        regroup_x(0)
+        w_grouped = consts.tile([P, D, PACK], BF16, align_bytes=64)
+        regroup(w_grouped[:], w_rows[:])
+        quantise_x(0)
+        w_codes = consts.tile([P, D], U32, align_bytes=64)
+        w_scales = consts.tile([P, D], U8, align_bytes=64)
+        nc.vector.quantize_mx(
+            out=w_codes[:].bitcast(FP8X4),
+            scales=w_scales[:],
+            in_=w_grouped[:].rearrange("p e t -> p (e t)"),
+        )
+
+        for it in range(N_SLABS + 4):
+            if live(it + AHEAD):
+                load_slab(it + AHEAD)
+            next_b = it // SLABS + 1
+            prepare_x = it % SLABS == SLABS - 2 and next_b < B
+            if live(it - 2):
+                quantise_merged(it - 2)
+            if live(it - 3):
+                add_residual(it - 3)
+            if live(it):
+                turn_head(it, 0)
+                quantise_head(it, 0)
+            if prepare_x:
+                regroup_x(next_b)
+            if live(it - 4):
+                finish(it - 4)
+            if live(it):
+                turn_head(it, 1)
+                quantise_head(it, 1)
+            if prepare_x:
+                quantise_x(next_b)
+            if live(it - 1):
+                pool_values(it - 1)
+            if live(it - 2):
+                project(it - 2)
+            if live(it - 3):
+                deviation(it - 3)

@@ -35,7 +35,7 @@ def tile_bertselfattention_pb_t_kernel(tc, probs, x, Wv, gamma, beta, out):
         consts = stack.enter_context(tc.tile_pool(name="consts", bufs=1))
         rows_pool = stack.enter_context(tc.tile_pool(name="rows", bufs=AHEAD + 1))
         x_pool = stack.enter_context(tc.tile_pool(name="x", bufs=2))
-        work = stack.enter_context(tc.tile_pool(name="work", bufs=2))
+        work = stack.enter_context(tc.tile_pool(name="work", bufs=3))
         norm = stack.enter_context(tc.tile_pool(name="norm", bufs=3))
         turn_banks = stack.enter_context(tc.psum_pool(name="turn_banks", bufs=4))
         ctx_banks = stack.enter_context(tc.psum_pool(name="ctx_banks", bufs=2))
@@ -44,7 +44,7 @@ def tile_bertselfattention_pb_t_kernel(tc, probs, x, Wv, gamma, beta, out):
 
         rows_of, grouped_of, codes_of, scales_of = {}, {}, {}, {}
         merged_of, m_codes_of, m_scales_of, y_of = {}, {}, {}, {}
-        yres_of, neg_mean_of, std_of, scaled_of = {}, {}, {}, {}
+        yres_of, neg_mean_of, rstd_of, scaled_of = {}, {}, {}, {}
         x_rows_of, x_grouped_of, x_codes_of, x_scales_of = {}, {}, {}, {}
 
         def load_slab(n):
@@ -80,8 +80,8 @@ def tile_bertselfattention_pb_t_kernel(tc, probs, x, Wv, gamma, beta, out):
             x_grouped_of[b] = x_grouped
 
         def quantise_x(b):
-            x_codes = x_pool.tile([P, PASSES * D], U32, align_bytes=64)
-            x_scales = x_pool.tile([P, PASSES * D], U8, align_bytes=64)
+            x_codes = x_pool.tile([P, PASSES * D], U32, align_bytes=64, bufs=B)
+            x_scales = x_pool.tile([P, PASSES * D], U8, align_bytes=64, bufs=B)
             nc.vector.quantize_mx(
                 out=x_codes[:].bitcast(FP8X4),
                 scales=x_scales[:],
@@ -113,17 +113,13 @@ def tile_bertselfattention_pb_t_kernel(tc, probs, x, Wv, gamma, beta, out):
                     out=grouped_words[:, h, g, :, :], in_=turned[:].rearrange("p u c -> p c u")
                 )
 
-        def quantise_head(n, h):
-            if h == 0:
-                codes = work.tile([P, H * HEAD_WORDS], U32, align_bytes=64)
-                scales = work.tile([P, H * HEAD_WORDS], U8, align_bytes=64)
-                codes_of[n], scales_of[n] = codes, scales
-            cols = slice(h * HEAD_WORDS, (h + 1) * HEAD_WORDS)
+        def quantise_slab(n):
+            codes = work.tile([P, H * HEAD_WORDS], U32, align_bytes=64)
+            scales = work.tile([P, H * HEAD_WORDS], U8, align_bytes=64)
             nc.vector.quantize_mx(
-                out=codes_of[n][:, cols].bitcast(FP8X4),
-                scales=scales_of[n][:, cols],
-                in_=grouped_of[n][:, h * HEAD_WORDS * PACK : (h + 1) * HEAD_WORDS * PACK],
+                out=codes[:].bitcast(FP8X4), scales=scales[:], in_=grouped_of[n][:]
             )
+            codes_of[n], scales_of[n] = codes, scales
 
         def pool_values(n):
             b = n // SLABS
@@ -176,7 +172,6 @@ def tile_bertselfattention_pb_t_kernel(tc, probs, x, Wv, gamma, beta, out):
             yres = norm.tile([P, ROW_PAIR, D], F32)
             row_sum = norm.tile([P, ROW_PAIR], F32)
             neg_mean = norm.tile([P, ROW_PAIR], F32)
-            scaled = norm.tile([P, ROW_PAIR, D], F32)
             for r in range(ROW_PAIR):
                 nc.vector.scalar_tensor_tensor(
                     out=yres[:, r, :],
@@ -187,23 +182,33 @@ def tile_bertselfattention_pb_t_kernel(tc, probs, x, Wv, gamma, beta, out):
                     op1=ALU.add,
                     accum_out=row_sum[:, r : r + 1],
                 )
-            nc.vector.tensor_scalar(
-                out=neg_mean[:], in0=row_sum[:], scalar1=-1.0 / D, scalar2=None, op0=ALU.mult
+            nc.gpsimd.tensor_scalar(
+                out=neg_mean[:],
+                in0=row_sum[:],
+                scalar1=-1.0 / D,
+                scalar2=0.0,
+                op0=ALU.mult,
+                op1=ALU.add,
             )
+            yres_of[n], neg_mean_of[n] = yres, neg_mean
+
+        def centre_and_gain(n):
+            scaled = norm.tile([P, ROW_PAIR, D], F32)
             for r in range(ROW_PAIR):
                 nc.vector.scalar_tensor_tensor(
                     out=scaled[:, r, :],
-                    in0=yres[:, r, :],
-                    scalar=neg_mean[:, r : r + 1],
+                    in0=yres_of[n][:, r, :],
+                    scalar=neg_mean_of[n][:, r : r + 1],
                     in1=gain_bias[:, 0, :],
                     op0=ALU.add,
                     op1=ALU.mult,
                 )
-            yres_of[n], neg_mean_of[n], scaled_of[n] = yres, neg_mean, scaled
+            scaled_of[n] = scaled
 
         def deviation(n):
             sq_sum = norm.tile([P, ROW_PAIR], F32)
-            std = norm.tile([P, ROW_PAIR], F32)
+            var_eps = norm.tile([P, ROW_PAIR], F32)
+            rstd = norm.tile([P, ROW_PAIR], F32)
             for r in range(ROW_PAIR):
                 squares = norm.tile([P, D], BF16)
                 nc.scalar.activation(
@@ -214,21 +219,25 @@ def tile_bertselfattention_pb_t_kernel(tc, probs, x, Wv, gamma, beta, out):
                     scale=1.0,
                     accum_out=sq_sum[:, r : r + 1],
                 )
-            nc.scalar.activation(
-                out=std[:], in_=sq_sum[:], func=ACT.Sqrt, bias=eps[:], scale=1.0 / D
+            nc.gpsimd.tensor_scalar(
+                out=var_eps[:],
+                in0=sq_sum[:],
+                scalar1=1.0 / D,
+                scalar2=LN_EPS,
+                op0=ALU.mult,
+                op1=ALU.add,
             )
-            std_of[n] = std
+            nc.gpsimd.tensor_tensor(out=rstd[:], in0=var_eps[:], in1=minus_half[:], op=ALU.pow)
+            rstd_of[n] = rstd
 
         def finish(n):
             b, a = divmod(n, SLABS)
-            rstd = norm.tile([P, ROW_PAIR], F32)
             result = norm.tile([P, ROW_PAIR, D], F32)
-            nc.vector.reciprocal(out=rstd[:], in_=std_of[n][:])
             for r in range(ROW_PAIR):
                 nc.vector.scalar_tensor_tensor(
                     out=result[:, r, :],
                     in0=scaled_of[n][:, r, :],
-                    scalar=rstd[:, r : r + 1],
+                    scalar=rstd_of[n][:, r : r + 1],
                     in1=gain_bias[:, 1, :],
                     op0=ALU.mult,
                     op1=ALU.add,
@@ -245,17 +254,15 @@ def tile_bertselfattention_pb_t_kernel(tc, probs, x, Wv, gamma, beta, out):
 
         ident = consts.tile([P, P], F32)
         make_identity(nc, ident[:])
-        eps = consts.tile([P, 1], F32)
-        nc.vector.memset(eps[:], LN_EPS)
-        first_table = consts.tile([P, 1], F32)
-        nc.scalar.activation(out=first_table[:], in_=eps[:], func=ACT.Sqrt)
+        minus_half = consts.tile([P, ROW_PAIR], F32)
+        nc.vector.memset(minus_half[:], -0.5)
 
         ones = consts.tile([P, P], BF16)
         nc.vector.memset(ones[:], 1.0)
         gb_row = consts.tile([P, 2, D], BF16)
         nc.vector.memset(gb_row[:], 0.0)
-        nc.scalar.dma_start(out=gb_row[0:1, 0, :], in_=gamma.rearrange("(o e) -> o e", o=1))
-        nc.scalar.dma_start(out=gb_row[0:1, 1, :], in_=beta.rearrange("(o e) -> o e", o=1))
+        nc.sync.dma_start(out=gb_row[0:1, 0, :], in_=gamma.rearrange("(o e) -> o e", o=1))
+        nc.sync.dma_start(out=gb_row[0:1, 1, :], in_=beta.rearrange("(o e) -> o e", o=1))
         gb_bank = y_banks.tile([P, 2, D], F32, tag="y")
         nc.tensor.matmul(
             out=gb_bank[:].rearrange("p k e -> p (k e)"),
@@ -275,10 +282,8 @@ def tile_bertselfattention_pb_t_kernel(tc, probs, x, Wv, gamma, beta, out):
             if n == 0:
                 nc.sync.dma_start(out=w_rows[:], in_=Wv.rearrange("(t p) e -> p t e", p=P))
 
-        regroup_x(0)
         w_grouped = consts.tile([P, D, PACK], BF16, align_bytes=64)
         regroup(w_grouped[:], w_rows[:])
-        quantise_x(0)
         w_codes = consts.tile([P, D], U32, align_bytes=64)
         w_scales = consts.tile([P, D], U8, align_bytes=64)
         nc.vector.quantize_mx(
@@ -290,24 +295,22 @@ def tile_bertselfattention_pb_t_kernel(tc, probs, x, Wv, gamma, beta, out):
         for it in range(N_SLABS + 4):
             if live(it + AHEAD):
                 load_slab(it + AHEAD)
-            next_b = it // SLABS + 1
-            prepare_x = it % SLABS == SLABS - 2 and next_b < B
-            if live(it - 2):
-                quantise_merged(it - 2)
+            if it < B:
+                regroup_x(it)
             if live(it - 3):
                 add_residual(it - 3)
-            if live(it):
-                turn_head(it, 0)
-                quantise_head(it, 0)
-            if prepare_x:
-                regroup_x(next_b)
+            if live(it - 2):
+                quantise_merged(it - 2)
             if live(it - 4):
                 finish(it - 4)
+            if it < B:
+                quantise_x(it)
+            if live(it - 3):
+                centre_and_gain(it - 3)
             if live(it):
+                turn_head(it, 0)
                 turn_head(it, 1)
-                quantise_head(it, 1)
-            if prepare_x:
-                quantise_x(next_b)
+                quantise_slab(it)
             if live(it - 1):
                 pool_values(it - 1)
             if live(it - 2):

@@ -43,7 +43,7 @@ def tile_bertselfattention_pb_t_kernel(tc, probs, x, Wv, gamma, beta, out):
         stack.enter_context(tc.manual_schedule())
 
         rows_of, grouped_of, codes_of, scales_of = {}, {}, {}, {}
-        merged_of, m_codes_of, m_scales_of, y_of = {}, {}, {}, {}
+        ctx_of, merged_of, m_codes_of, m_scales_of, y_of = {}, {}, {}, {}, {}
         yres_of, neg_mean_of, rstd_of, scaled_of = {}, {}, {}, {}
         x_rows_of, x_grouped_of, x_codes_of, x_scales_of = {}, {}, {}, {}
 
@@ -121,26 +121,32 @@ def tile_bertselfattention_pb_t_kernel(tc, probs, x, Wv, gamma, beta, out):
             )
             codes_of[n], scales_of[n] = codes, scales
 
-        def pool_values(n):
+        def pool_head(n, h):
             b = n // SLABS
+            for r in range(ROW_PAIR):
+                if h == 0:
+                    ctx_t = ctx_banks.tile([P, PACK, P], F32)
+                    ctx_of[n, r] = ctx_t
+                for half in range(HALVES):
+                    for g in range(PASSES):
+                        x_cols = slice(g * D + half * P, g * D + (half + 1) * P)
+                        first = h * HEAD_WORDS + g * SLAB + r * P
+                        nc.tensor.matmul_mx(
+                            out=ctx_of[n, r][:, h * HALVES + half, :],
+                            lhsT=x_codes_of[b][:, x_cols].bitcast(FP8X4),
+                            lhsT_scale=x_scales_of[b][:, x_cols],
+                            rhs=codes_of[n][:, first : first + P].bitcast(FP8X4),
+                            rhs_scale=scales_of[n][:, first : first + P],
+                            start=(g == 0),
+                            stop=(g == PASSES - 1),
+                        )
+
+        def merge_heads(n):
             merged = work.tile([P, ROW_PAIR, P, PACK], BF16, align_bytes=64)
             for r in range(ROW_PAIR):
-                ctx_t = ctx_banks.tile([P, PACK, P], F32)
-                for h in range(H):
-                    for half in range(HALVES):
-                        for g in range(PASSES):
-                            x_cols = slice(g * D + half * P, g * D + (half + 1) * P)
-                            first = h * HEAD_WORDS + g * SLAB + r * P
-                            nc.tensor.matmul_mx(
-                                out=ctx_t[:, h * HALVES + half, :],
-                                lhsT=x_codes_of[b][:, x_cols].bitcast(FP8X4),
-                                lhsT_scale=x_scales_of[b][:, x_cols],
-                                rhs=codes_of[n][:, first : first + P].bitcast(FP8X4),
-                                rhs_scale=scales_of[n][:, first : first + P],
-                                start=(g == 0),
-                                stop=(g == PASSES - 1),
-                            )
-                nc.scalar.copy(out=merged[:, r, :, :], in_=ctx_t[:].rearrange("p t i -> p i t"))
+                nc.scalar.copy(
+                    out=merged[:, r, :, :], in_=ctx_of[n, r][:].rearrange("p t i -> p i t")
+                )
             merged_of[n] = merged
 
         def quantise_merged(n):
@@ -307,12 +313,15 @@ def tile_bertselfattention_pb_t_kernel(tc, probs, x, Wv, gamma, beta, out):
                 quantise_x(it)
             if live(it - 3):
                 centre_and_gain(it - 3)
+            for h in range(H):
+                if live(it):
+                    turn_head(it, h)
+                if live(it - 1):
+                    pool_head(it - 1, h)
             if live(it):
-                turn_head(it, 0)
-                turn_head(it, 1)
                 quantise_slab(it)
             if live(it - 1):
-                pool_values(it - 1)
+                merge_heads(it - 1)
             if live(it - 2):
                 project(it - 2)
             if live(it - 3):

@@ -36,15 +36,15 @@ def tile_bertselfattention_pb_t_kernel(tc, probs, x, Wv, gamma, beta, out):
         rows_pool = stack.enter_context(tc.tile_pool(name="rows", bufs=AHEAD + 1))
         x_pool = stack.enter_context(tc.tile_pool(name="x", bufs=2))
         work = stack.enter_context(tc.tile_pool(name="work", bufs=3))
-        norm = stack.enter_context(tc.tile_pool(name="norm", bufs=3))
+        norm = stack.enter_context(tc.tile_pool(name="norm", bufs=4))
         turn_banks = stack.enter_context(tc.psum_pool(name="turn_banks", bufs=4))
         ctx_banks = stack.enter_context(tc.psum_pool(name="ctx_banks", bufs=2))
         y_banks = stack.enter_context(tc.psum_pool(name="y_banks", bufs=2))
         stack.enter_context(tc.manual_schedule())
 
         rows_of, grouped_of, codes_of, scales_of = {}, {}, {}, {}
-        ctx_of, merged_of, m_codes_of, m_scales_of, y_of = {}, {}, {}, {}, {}
-        yres_of, neg_mean_of, rstd_of, scaled_of = {}, {}, {}, {}
+        merged_of, m_codes_of, m_scales_of, y_of = {}, {}, {}, {}
+        yres_of, row_sum_of, neg_mean_of, rstd_of, scaled_of = {}, {}, {}, {}, {}
         x_rows_of, x_grouped_of, x_codes_of, x_scales_of = {}, {}, {}, {}
 
         def load_slab(n):
@@ -121,32 +121,30 @@ def tile_bertselfattention_pb_t_kernel(tc, probs, x, Wv, gamma, beta, out):
             )
             codes_of[n], scales_of[n] = codes, scales
 
-        def pool_head(n, h):
+        def pool_values(n):
             b = n // SLABS
-            for r in range(ROW_PAIR):
-                if h == 0:
-                    ctx_t = ctx_banks.tile([P, PACK, P], F32)
-                    ctx_of[n, r] = ctx_t
-                for half in range(HALVES):
-                    for g in range(PASSES):
-                        x_cols = slice(g * D + half * P, g * D + (half + 1) * P)
-                        first = h * HEAD_WORDS + g * SLAB + r * P
-                        nc.tensor.matmul_mx(
-                            out=ctx_of[n, r][:, h * HALVES + half, :],
-                            lhsT=x_codes_of[b][:, x_cols].bitcast(FP8X4),
-                            lhsT_scale=x_scales_of[b][:, x_cols],
-                            rhs=codes_of[n][:, first : first + P].bitcast(FP8X4),
-                            rhs_scale=scales_of[n][:, first : first + P],
-                            start=(g == 0),
-                            stop=(g == PASSES - 1),
-                        )
-
-        def merge_heads(n):
             merged = work.tile([P, ROW_PAIR, P, PACK], BF16, align_bytes=64)
             for r in range(ROW_PAIR):
-                nc.scalar.copy(
-                    out=merged[:, r, :, :], in_=ctx_of[n, r][:].rearrange("p t i -> p i t")
-                )
+                ctx_t = ctx_banks.tile([P, PACK, P], F32)
+                for h in range(H):
+                    for half in range(HALVES):
+                        for g in range(PASSES):
+                            x_cols = slice(g * D + half * P, g * D + (half + 1) * P)
+                            first = h * HEAD_WORDS + g * SLAB + r * P
+                            nc.tensor.matmul_mx(
+                                out=ctx_t[:, h * HALVES + half, :],
+                                lhsT=x_codes_of[b][:, x_cols].bitcast(FP8X4),
+                                lhsT_scale=x_scales_of[b][:, x_cols],
+                                rhs=codes_of[n][:, first : first + P].bitcast(FP8X4),
+                                rhs_scale=scales_of[n][:, first : first + P],
+                                start=(g == 0),
+                                stop=(g == PASSES - 1),
+                            )
+                if n % 2 == 1 and r == 1:
+                    copy_out = nc.vector.tensor_copy
+                else:
+                    copy_out = nc.scalar.copy
+                copy_out(out=merged[:, r, :, :], in_=ctx_t[:].rearrange("p t i -> p i t"))
             merged_of[n] = merged
 
         def quantise_merged(n):
@@ -177,7 +175,6 @@ def tile_bertselfattention_pb_t_kernel(tc, probs, x, Wv, gamma, beta, out):
             b, a = divmod(n, SLABS)
             yres = norm.tile([P, ROW_PAIR, D], F32)
             row_sum = norm.tile([P, ROW_PAIR], F32)
-            neg_mean = norm.tile([P, ROW_PAIR], F32)
             for r in range(ROW_PAIR):
                 nc.vector.scalar_tensor_tensor(
                     out=yres[:, r, :],
@@ -188,15 +185,14 @@ def tile_bertselfattention_pb_t_kernel(tc, probs, x, Wv, gamma, beta, out):
                     op1=ALU.add,
                     accum_out=row_sum[:, r : r + 1],
                 )
-            nc.gpsimd.tensor_scalar(
-                out=neg_mean[:],
-                in0=row_sum[:],
-                scalar1=-1.0 / D,
-                scalar2=0.0,
-                op0=ALU.mult,
-                op1=ALU.add,
+            yres_of[n], row_sum_of[n] = yres, row_sum
+
+        def negate_mean(n):
+            neg_mean = norm.tile([P, ROW_PAIR], F32)
+            nc.vector.tensor_scalar(
+                out=neg_mean[:], in0=row_sum_of[n][:], scalar1=-1.0 / D, scalar2=None, op0=ALU.mult
             )
-            yres_of[n], neg_mean_of[n] = yres, neg_mean
+            neg_mean_of[n] = neg_mean
 
         def centre_and_gain(n):
             scaled = norm.tile([P, ROW_PAIR, D], F32)
@@ -298,7 +294,7 @@ def tile_bertselfattention_pb_t_kernel(tc, probs, x, Wv, gamma, beta, out):
             in_=w_grouped[:].rearrange("p e t -> p (e t)"),
         )
 
-        for it in range(N_SLABS + 4):
+        for it in range(N_SLABS + 5):
             if live(it + AHEAD):
                 load_slab(it + AHEAD)
             if it < B:
@@ -307,21 +303,20 @@ def tile_bertselfattention_pb_t_kernel(tc, probs, x, Wv, gamma, beta, out):
                 add_residual(it - 3)
             if live(it - 2):
                 quantise_merged(it - 2)
-            if live(it - 4):
-                finish(it - 4)
+            if live(it - 3):
+                negate_mean(it - 3)
+            if live(it - 5):
+                finish(it - 5)
             if it < B:
                 quantise_x(it)
             if live(it - 3):
                 centre_and_gain(it - 3)
-            for h in range(H):
-                if live(it):
-                    turn_head(it, h)
-                if live(it - 1):
-                    pool_head(it - 1, h)
             if live(it):
+                turn_head(it, 0)
+                turn_head(it, 1)
                 quantise_slab(it)
             if live(it - 1):
-                merge_heads(it - 1)
+                pool_values(it - 1)
             if live(it - 2):
                 project(it - 2)
             if live(it - 3):

@@ -16,6 +16,7 @@ LN_EPS = 1e-5
 FLOPS = 2 * B * H * S * S * D + 2 * B * S * (H * D) * D
 
 P = 128
+BANK = 512
 PACK = 4
 PASSES = S // (P * PACK)
 TURNS = 2
@@ -23,10 +24,16 @@ ROW_PAIR = 2
 SLAB = P * ROW_PAIR
 SLABS = S // SLAB
 N_SLABS = B * SLABS
+UNITS = N_SLABS * ROW_PAIR
 HALVES = D // P
-HEAD_WORDS = PASSES * SLAB
-AHEAD = 4
-assert AHEAD >= B
+COLS = H * P
+AHEAD = 6
+X_STEPS = PASSES + 1
+LAG = {"T": 0, "Q": 1, "M": 2, "K": 3, "Y": 3, "R": 4, "N": 4, "H": 5, "D": 4, "F": 6}
+ORDER = "TRQMKYFNHD"
+X_LOAD = {1: 1, 2: 4, 3: 7}
+X_AT = {1: (2, 3, 4), 2: (7, 10, 13), 3: (16, 19, 22)}
+W_AT = 1
 
 
 def tile_bertselfattention_pb_t_kernel(tc, probs, x, Wv, gamma, beta, out):
@@ -35,29 +42,39 @@ def tile_bertselfattention_pb_t_kernel(tc, probs, x, Wv, gamma, beta, out):
         consts = stack.enter_context(tc.tile_pool(name="consts", bufs=1))
         rows_pool = stack.enter_context(tc.tile_pool(name="rows", bufs=AHEAD + 1))
         x_pool = stack.enter_context(tc.tile_pool(name="x", bufs=2))
-        work = stack.enter_context(tc.tile_pool(name="work", bufs=3))
+        work = stack.enter_context(tc.tile_pool(name="work", bufs=4))
         norm = stack.enter_context(tc.tile_pool(name="norm", bufs=4))
         turn_banks = stack.enter_context(tc.psum_pool(name="turn_banks", bufs=4))
         ctx_banks = stack.enter_context(tc.psum_pool(name="ctx_banks", bufs=2))
         y_banks = stack.enter_context(tc.psum_pool(name="y_banks", bufs=2))
         stack.enter_context(tc.manual_schedule())
 
-        rows_of, grouped_of, codes_of, scales_of = {}, {}, {}, {}
+        rows_of, x_rows_of, x_grouped_of, x_codes_of, x_scales_of = {}, {}, {}, {}, {}
+        grouped_of, codes_of, scales_of = {}, {}, {}
         merged_of, m_codes_of, m_scales_of, y_of = {}, {}, {}, {}
-        yres_of, row_sum_of, neg_mean_of, rstd_of, scaled_of = {}, {}, {}, {}, {}
-        x_rows_of, x_grouped_of, x_codes_of, x_scales_of = {}, {}, {}, {}
+        yres_of, row_sum_of, neg_mean_of, rstd_of, scaled_of, result_of = {}, {}, {}, {}, {}, {}
 
-        def load_slab(n):
+        def probs_rows(n, h):
             b, a = divmod(n, SLABS)
-            rows = rows_pool.tile([P, H * ROW_PAIR * S], BF16)
+            return probs[b, h, a * SLAB : (a + 1) * SLAB, :]
+
+        def new_rows(n):
+            rows_of[n] = rows_pool.tile([P, H, ROW_PAIR, S], BF16, name="rows")
+
+        def load_unit(n, r):
             for h in range(H):
                 nc.sync.dma_start(
-                    out=rows[:, h * ROW_PAIR * S : (h + 1) * ROW_PAIR * S],
-                    in_=probs[b, h, a * SLAB : (a + 1) * SLAB, :].rearrange(
-                        "(p r) j -> p (r j)", r=ROW_PAIR
-                    ),
+                    out=rows_of[n][:, h, r, :],
+                    in_=probs_rows(n, h).rearrange("(p r) j -> r p j", r=ROW_PAIR)[r],
                 )
-            rows_of[n] = rows
+
+        def load_slab(n):
+            new_rows(n)
+            for h in range(H):
+                nc.sync.dma_start(
+                    out=rows_of[n][:, h, :, :].rearrange("p r j -> p (r j)"),
+                    in_=probs_rows(n, h).rearrange("(p r) j -> p (r j)", r=ROW_PAIR),
+                )
 
         def load_x(b):
             x_rows = x_pool.tile([P, SLABS * ROW_PAIR, D], BF16, bufs=B)
@@ -73,11 +90,12 @@ def tile_bertselfattention_pb_t_kernel(tc, probs, x, Wv, gamma, beta, out):
                 in_=planes.rearrange("p t (c i) -> p c t i", i=4),
             )
 
-        def regroup_x(b):
-            x_grouped = x_pool.tile([P, PASSES, D, PACK], BF16, align_bytes=64)
-            for g in range(PASSES):
-                regroup(x_grouped[:, g, :, :], x_rows_of[b][:, g * PACK : (g + 1) * PACK, :])
-            x_grouped_of[b] = x_grouped
+        def regroup_x(b, g):
+            if g == 0:
+                x_grouped_of[b] = x_pool.tile(
+                    [P, PASSES, D, PACK], BF16, align_bytes=64, name="x_grouped"
+                )
+            regroup(x_grouped_of[b][:, g, :, :], x_rows_of[b][:, g * PACK : (g + 1) * PACK, :])
 
         def quantise_x(b):
             x_codes = x_pool.tile([P, PASSES * D], U32, align_bytes=64, bufs=B)
@@ -89,138 +107,132 @@ def tile_bertselfattention_pb_t_kernel(tc, probs, x, Wv, gamma, beta, out):
             )
             x_codes_of[b], x_scales_of[b] = x_codes, x_scales
 
-        def turn_head(n, h):
-            if h == 0:
-                grouped = work.tile([P, H * HEAD_WORDS * PACK], BF16, align_bytes=64)
-                grouped_of[n] = grouped
-            words = rows_of[n][:].bitcast(F32).rearrange(
-                "p (h r w) -> p h r w", h=H, r=ROW_PAIR
+        def prepare_x(b, steps):
+            for step in steps:
+                if step < PASSES:
+                    regroup_x(b, step)
+                else:
+                    quantise_x(b)
+
+        def turn_unit(m):
+            n, r = divmod(m, ROW_PAIR)
+            grouped = work.tile([P, PASSES * COLS * PACK], BF16, align_bytes=64)
+            grouped_of[m] = grouped
+            grouped_words = grouped[:].bitcast(F32).rearrange(
+                "p (g h c u) -> p g h c u", g=PASSES, h=H, u=TURNS
             )
-            grouped_words = grouped_of[n][:].bitcast(F32).rearrange(
-                "p (h g c u) -> p h g c u", h=H, g=PASSES, u=TURNS
-            )
-            for g in range(PASSES):
-                turned = turn_banks.tile([P, TURNS, SLAB], F32)
-                for u in range(TURNS):
-                    first = (g * TURNS + u) * P
-                    for r in range(ROW_PAIR):
+            for h in range(H):
+                words = rows_of[n][:, h, r, :].bitcast(F32)
+                turned = turn_banks.tile([P, PASSES, TURNS, P], F32)
+                for g in range(PASSES):
+                    for u in range(TURNS):
+                        first = (g * TURNS + u) * P
                         nc.tensor.transpose(
-                            turned[:, u, r * P : (r + 1) * P],
-                            words[:, h, r, first : first + P],
-                            ident[:],
+                            turned[:, g, u, :], words[:, first : first + P], ident[:]
                         )
                 nc.scalar.copy(
-                    out=grouped_words[:, h, g, :, :], in_=turned[:].rearrange("p u c -> p c u")
+                    out=grouped_words[:, :, h, :, :],
+                    in_=turned[:].rearrange("p g u c -> p g c u"),
                 )
 
-        def quantise_slab(n):
-            codes = work.tile([P, H * HEAD_WORDS], U32, align_bytes=64)
-            scales = work.tile([P, H * HEAD_WORDS], U8, align_bytes=64)
+        def quantise_unit(m):
+            codes = work.tile([P, PASSES * COLS], U32, align_bytes=64)
+            scales = work.tile([P, PASSES * COLS], U8, align_bytes=64)
             nc.vector.quantize_mx(
-                out=codes[:].bitcast(FP8X4), scales=scales[:], in_=grouped_of[n][:]
+                out=codes[:].bitcast(FP8X4), scales=scales[:], in_=grouped_of[m][:]
             )
-            codes_of[n], scales_of[n] = codes, scales
+            codes_of[m], scales_of[m] = codes, scales
 
-        def pool_values(n):
-            b = n // SLABS
-            merged = work.tile([P, ROW_PAIR, P, PACK], BF16, align_bytes=64)
-            for r in range(ROW_PAIR):
-                ctx_t = ctx_banks.tile([P, PACK, P], F32)
-                for h in range(H):
-                    for half in range(HALVES):
-                        for g in range(PASSES):
-                            x_cols = slice(g * D + half * P, g * D + (half + 1) * P)
-                            first = h * HEAD_WORDS + g * SLAB + r * P
-                            nc.tensor.matmul_mx(
-                                out=ctx_t[:, h * HALVES + half, :],
-                                lhsT=x_codes_of[b][:, x_cols].bitcast(FP8X4),
-                                lhsT_scale=x_scales_of[b][:, x_cols],
-                                rhs=codes_of[n][:, first : first + P].bitcast(FP8X4),
-                                rhs_scale=scales_of[n][:, first : first + P],
-                                start=(g == 0),
-                                stop=(g == PASSES - 1),
-                            )
-                if n % 2 == 1 and r == 1:
-                    copy_out = nc.vector.tensor_copy
-                else:
-                    copy_out = nc.scalar.copy
-                copy_out(out=merged[:, r, :, :], in_=ctx_t[:].rearrange("p t i -> p i t"))
-            merged_of[n] = merged
+        def pool_values(m):
+            b = m // (SLABS * ROW_PAIR)
+            ctx_t = ctx_banks.tile([P, PACK, P], F32)
+            for f in range(HALVES):
+                for g in range(PASSES):
+                    x_cols = slice(g * D + f * P, g * D + (f + 1) * P)
+                    q_cols = slice(g * COLS, (g + 1) * COLS)
+                    nc.tensor.matmul_mx(
+                        out=ctx_t[:, f * H : (f + 1) * H, :].rearrange("p h c -> p (h c)"),
+                        lhsT=x_codes_of[b][:, x_cols].bitcast(FP8X4),
+                        lhsT_scale=x_scales_of[b][:, x_cols],
+                        rhs=codes_of[m][:, q_cols].bitcast(FP8X4),
+                        rhs_scale=scales_of[m][:, q_cols],
+                        start=(g == 0),
+                        stop=(g == PASSES - 1),
+                    )
+            merged = work.tile([P, P, PACK], BF16, align_bytes=64)
+            nc.scalar.copy(out=merged[:], in_=ctx_t[:].rearrange("p t c -> p c t"))
+            merged_of[m] = merged
 
-        def quantise_merged(n):
-            m_codes = work.tile([P, SLAB], U32, align_bytes=64)
-            m_scales = work.tile([P, SLAB], U8, align_bytes=64)
+        def quantise_merged(m):
+            m_codes = work.tile([P, P], U32, align_bytes=64)
+            m_scales = work.tile([P, P], U8, align_bytes=64)
             nc.vector.quantize_mx(
                 out=m_codes[:].bitcast(FP8X4),
                 scales=m_scales[:],
-                in_=merged_of[n][:].rearrange("p r i t -> p (r i t)"),
+                in_=merged_of[m][:].rearrange("p c t -> p (c t)"),
             )
-            m_codes_of[n], m_scales_of[n] = m_codes, m_scales
+            m_codes_of[m], m_scales_of[m] = m_codes, m_scales
 
-        def project(n):
-            y = y_banks.tile([P, ROW_PAIR, D], F32)
-            for r in range(ROW_PAIR):
-                nc.tensor.matmul_mx(
-                    out=y[:, r, :],
-                    lhsT=m_codes_of[n][:, r * P : (r + 1) * P].bitcast(FP8X4),
-                    lhsT_scale=m_scales_of[n][:, r * P : (r + 1) * P],
-                    rhs=w_codes[:].bitcast(FP8X4),
-                    rhs_scale=w_scales[:],
-                    start=True,
-                    stop=True,
-                )
-            y_of[n] = y
+        def project(m):
+            y = y_banks.tile([P, BANK], F32)
+            nc.tensor.matmul_mx(
+                out=y[:, :D],
+                lhsT=m_codes_of[m][:].bitcast(FP8X4),
+                lhsT_scale=m_scales_of[m][:],
+                rhs=w_codes[:].bitcast(FP8X4),
+                rhs_scale=w_scales[:],
+                start=True,
+                stop=True,
+            )
+            y_of[m] = y
 
-        def add_residual(n):
-            b, a = divmod(n, SLABS)
-            yres = norm.tile([P, ROW_PAIR, D], F32)
-            row_sum = norm.tile([P, ROW_PAIR], F32)
-            for r in range(ROW_PAIR):
-                nc.vector.scalar_tensor_tensor(
-                    out=yres[:, r, :],
-                    in0=y_of[n][:, r, :],
-                    scalar=1.0,
-                    in1=x_rows_of[b][:, a * ROW_PAIR + r, :],
-                    op0=ALU.mult,
-                    op1=ALU.add,
-                    accum_out=row_sum[:, r : r + 1],
-                )
-            yres_of[n], row_sum_of[n] = yres, row_sum
+        def add_residual(m):
+            b, q = divmod(m, SLABS * ROW_PAIR)
+            yres = norm.tile([P, D], F32)
+            row_sum = norm.tile([P, 1], F32)
+            nc.vector.scalar_tensor_tensor(
+                out=yres[:],
+                in0=y_of[m][:, :D],
+                scalar=1.0,
+                in1=x_rows_of[b][:, q, :],
+                op0=ALU.mult,
+                op1=ALU.add,
+                accum_out=row_sum[:],
+            )
+            yres_of[m], row_sum_of[m] = yres, row_sum
 
-        def negate_mean(n):
-            neg_mean = norm.tile([P, ROW_PAIR], F32)
+        def negate_mean(m):
+            neg_mean = norm.tile([P, 1], F32)
             nc.vector.tensor_scalar(
-                out=neg_mean[:], in0=row_sum_of[n][:], scalar1=-1.0 / D, scalar2=None, op0=ALU.mult
+                out=neg_mean[:], in0=row_sum_of[m][:], scalar1=-1.0 / D, scalar2=None, op0=ALU.mult
             )
-            neg_mean_of[n] = neg_mean
+            neg_mean_of[m] = neg_mean
 
-        def centre_and_gain(n):
-            scaled = norm.tile([P, ROW_PAIR, D], F32)
-            for r in range(ROW_PAIR):
-                nc.vector.scalar_tensor_tensor(
-                    out=scaled[:, r, :],
-                    in0=yres_of[n][:, r, :],
-                    scalar=neg_mean_of[n][:, r : r + 1],
-                    in1=gain_bias[:, 0, :],
-                    op0=ALU.add,
-                    op1=ALU.mult,
-                )
-            scaled_of[n] = scaled
+        def centre_and_gain(m):
+            scaled = norm.tile([P, D], F32)
+            nc.vector.scalar_tensor_tensor(
+                out=scaled[:],
+                in0=yres_of[m][:],
+                scalar=neg_mean_of[m][:],
+                in1=gain_bias[:, 0, :],
+                op0=ALU.add,
+                op1=ALU.mult,
+            )
+            scaled_of[m] = scaled
 
-        def deviation(n):
-            sq_sum = norm.tile([P, ROW_PAIR], F32)
-            var_eps = norm.tile([P, ROW_PAIR], F32)
-            rstd = norm.tile([P, ROW_PAIR], F32)
-            for r in range(ROW_PAIR):
-                squares = norm.tile([P, D], BF16)
-                nc.scalar.activation(
-                    out=squares[:],
-                    in_=yres_of[n][:, r, :],
-                    func=ACT.Square,
-                    bias=neg_mean_of[n][:, r : r + 1],
-                    scale=1.0,
-                    accum_out=sq_sum[:, r : r + 1],
-                )
+        def deviation(m):
+            sq_sum = norm.tile([P, 1], F32)
+            var_eps = norm.tile([P, 1], F32)
+            rstd = norm.tile([P, 1], F32)
+            squares = norm.tile([P, D], BF16)
+            nc.scalar.activation(
+                out=squares[:],
+                in_=yres_of[m][:],
+                func=ACT.Square,
+                bias=neg_mean_of[m][:],
+                scale=1.0,
+                accum_out=sq_sum[:],
+            )
             nc.gpsimd.tensor_scalar(
                 out=var_eps[:],
                 in0=sq_sum[:],
@@ -230,94 +242,109 @@ def tile_bertselfattention_pb_t_kernel(tc, probs, x, Wv, gamma, beta, out):
                 op1=ALU.add,
             )
             nc.gpsimd.tensor_tensor(out=rstd[:], in0=var_eps[:], in1=minus_half[:], op=ALU.pow)
-            rstd_of[n] = rstd
+            rstd_of[m] = rstd
 
-        def finish(n):
+        def finish(m):
+            n, r = divmod(m, ROW_PAIR)
             b, a = divmod(n, SLABS)
-            result = norm.tile([P, ROW_PAIR, D], F32)
-            for r in range(ROW_PAIR):
-                nc.vector.scalar_tensor_tensor(
-                    out=result[:, r, :],
-                    in0=scaled_of[n][:, r, :],
-                    scalar=rstd_of[n][:, r : r + 1],
-                    in1=gain_bias[:, 1, :],
-                    op0=ALU.mult,
-                    op1=ALU.add,
-                )
-            nc.sync.dma_start(
-                out=out[b, a * SLAB : (a + 1) * SLAB, :].rearrange(
-                    "(p r) e -> p r e", r=ROW_PAIR
-                ),
-                in_=result[:],
+            if r == 0:
+                result_of[n] = norm.tile([P, ROW_PAIR, D], F32, name="result")
+            nc.vector.scalar_tensor_tensor(
+                out=result_of[n][:, r, :],
+                in0=scaled_of[m][:],
+                scalar=rstd_of[m][:],
+                in1=gain_bias[:, 1, :],
+                op0=ALU.mult,
+                op1=ALU.add,
             )
-
-        def live(n):
-            return 0 <= n < N_SLABS
+            rows = out[b, a * SLAB : (a + 1) * SLAB, :].rearrange("(p r) e -> p r e", r=ROW_PAIR)
+            if n == N_SLABS - 1:
+                nc.sync.dma_start(out=rows[:, r, :], in_=result_of[n][:, r, :])
+            elif r == ROW_PAIR - 1:
+                nc.sync.dma_start(out=rows, in_=result_of[n][:])
 
         ident = consts.tile([P, P], F32)
         make_identity(nc, ident[:])
-        minus_half = consts.tile([P, ROW_PAIR], F32)
+        minus_half = consts.tile([P, 1], F32)
         nc.vector.memset(minus_half[:], -0.5)
-
         ones = consts.tile([P, P], BF16)
         nc.vector.memset(ones[:], 1.0)
         gb_row = consts.tile([P, 2, D], BF16)
         nc.vector.memset(gb_row[:], 0.0)
-        nc.sync.dma_start(out=gb_row[0:1, 0, :], in_=gamma.rearrange("(o e) -> o e", o=1))
-        nc.sync.dma_start(out=gb_row[0:1, 1, :], in_=beta.rearrange("(o e) -> o e", o=1))
-        gb_bank = y_banks.tile([P, 2, D], F32, tag="y")
-        nc.tensor.matmul(
-            out=gb_bank[:].rearrange("p k e -> p (k e)"),
-            lhsT=ones[:],
-            rhs=gb_row[:].rearrange("p k e -> p (k e)"),
-            start=True,
-            stop=True,
-        )
         gain_bias = consts.tile([P, 2, D], F32)
-        nc.scalar.copy(out=gain_bias[:], in_=gb_bank[:])
-
         w_rows = consts.tile([P, PACK, D], BF16)
-        for n in range(AHEAD):
-            load_slab(n)
-            if n < B:
-                load_x(n)
-            if n == 0:
-                nc.sync.dma_start(out=w_rows[:], in_=Wv.rearrange("(t p) e -> p t e", p=P))
-
         w_grouped = consts.tile([P, D, PACK], BF16, align_bytes=64)
-        regroup(w_grouped[:], w_rows[:])
         w_codes = consts.tile([P, D], U32, align_bytes=64)
         w_scales = consts.tile([P, D], U8, align_bytes=64)
-        nc.vector.quantize_mx(
-            out=w_codes[:].bitcast(FP8X4),
-            scales=w_scales[:],
-            in_=w_grouped[:].rearrange("p e t -> p (e t)"),
-        )
 
-        for it in range(N_SLABS + 5):
-            if live(it + AHEAD):
-                load_slab(it + AHEAD)
-            if it < B:
-                regroup_x(it)
-            if live(it - 3):
-                add_residual(it - 3)
-            if live(it - 2):
-                quantise_merged(it - 2)
-            if live(it - 3):
-                negate_mean(it - 3)
-            if live(it - 5):
-                finish(it - 5)
-            if it < B:
-                quantise_x(it)
-            if live(it - 3):
-                centre_and_gain(it - 3)
-            if live(it):
-                turn_head(it, 0)
-                turn_head(it, 1)
-                quantise_slab(it)
-            if live(it - 1):
-                pool_values(it - 1)
-            if live(it - 2):
-                project(it - 2)
-            if live(it - 3):
-                deviation(it - 3)
+        def load_weights():
+            for f in range(HALVES):
+                nc.sync.dma_start(
+                    out=w_rows[:, f * H : (f + 1) * H, :],
+                    in_=Wv.rearrange("(h f p) e -> f p h e", h=H, f=HALVES)[f],
+                )
+            nc.sync.dma_start(out=gb_row[0:1, 0, :], in_=gamma.rearrange("(o e) -> o e", o=1))
+            nc.sync.dma_start(out=gb_row[0:1, 1, :], in_=beta.rearrange("(o e) -> o e", o=1))
+
+        def prepare_weights():
+            regroup(w_grouped[:], w_rows[:])
+            nc.vector.quantize_mx(
+                out=w_codes[:].bitcast(FP8X4),
+                scales=w_scales[:],
+                in_=w_grouped[:].rearrange("p e t -> p (e t)"),
+            )
+
+        def spread_gain_bias():
+            gb_bank = y_banks.tile([P, BANK], F32, tag="y")
+            nc.tensor.matmul(
+                out=gb_bank[:],
+                lhsT=ones[:],
+                rhs=gb_row[:].rearrange("p k e -> p (k e)"),
+                start=True,
+                stop=True,
+            )
+            nc.scalar.copy(out=gain_bias[:].rearrange("p k e -> p (k e)"), in_=gb_bank[:])
+
+        new_rows(0)
+        load_unit(0, 0)
+        load_x(0)
+        load_unit(0, 1)
+        load_weights()
+        def load_slab_and_x(n):
+            load_slab(n)
+            for b in range(1, B):
+                if X_LOAD[b] == n:
+                    load_x(b)
+
+        for n in range(1, AHEAD):
+            load_slab_and_x(n)
+
+        def live(m):
+            return 0 <= m < UNITS
+
+        stages = {
+            "T": turn_unit,
+            "Q": quantise_unit,
+            "M": pool_values,
+            "K": quantise_merged,
+            "Y": project,
+            "R": add_residual,
+            "N": negate_mean,
+            "H": centre_and_gain,
+            "D": deviation,
+            "F": finish,
+        }
+        for it in range(UNITS + max(LAG.values())):
+            if it % ROW_PAIR == 0 and it // ROW_PAIR + AHEAD < N_SLABS:
+                load_slab_and_x(it // ROW_PAIR + AHEAD)
+            for key in ORDER:
+                if live(it - LAG[key]):
+                    stages[key](it - LAG[key])
+                if key == "T" and it == 0:
+                    prepare_x(0, range(X_STEPS))
+            if it == W_AT:
+                prepare_weights()
+                spread_gain_bias()
+            for b in range(1, B):
+                if it in X_AT[b]:
+                    prepare_x(b, [X_AT[b].index(it)])

@@ -29,7 +29,7 @@ HALVES = D // P
 COLS = H * P
 AHEAD = 6
 X_STEPS = PASSES + 1
-LAG = {"T": 0, "Q": 1, "M": 2, "K": 3, "Y": 3, "R": 4, "N": 4, "H": 5, "D": 4, "F": 6}
+LAG = {"T": 0, "Q": 1, "M": 2, "K": 3, "Y": 3, "R": 4, "N": 4, "H": 5, "D": 4, "F": 7}
 ORDER = "TRQMKYFNHD"
 X_LOAD = {1: 1, 2: 4, 3: 7}
 X_AT = {1: (2, 3, 4), 2: (7, 10, 13), 3: (16, 19, 22)}
@@ -52,7 +52,7 @@ def tile_bertselfattention_pb_t_kernel(tc, probs, x, Wv, gamma, beta, out):
         rows_of, x_rows_of, x_grouped_of, x_codes_of, x_scales_of = {}, {}, {}, {}, {}
         grouped_of, codes_of, scales_of = {}, {}, {}
         merged_of, m_codes_of, m_scales_of, y_of = {}, {}, {}, {}
-        yres_of, row_sum_of, neg_mean_of, rstd_of, scaled_of, result_of = {}, {}, {}, {}, {}, {}
+        yres_of, row_sum_of, neg_mean_of, rstd_of, scaled_of, result_of, sq_sum_of = {}, {}, {}, {}, {}, {}, {}
 
         def probs_rows(n, h):
             b, a = divmod(n, SLABS)
@@ -221,9 +221,9 @@ def tile_bertselfattention_pb_t_kernel(tc, probs, x, Wv, gamma, beta, out):
             scaled_of[m] = scaled
 
         def deviation(m):
-            sq_sum = norm.tile([P, 1], F32)
-            var_eps = norm.tile([P, 1], F32)
-            rstd = norm.tile([P, 1], F32)
+            n, r = divmod(m, ROW_PAIR)
+            if r == 0:
+                sq_sum_of[n] = norm.tile([P, ROW_PAIR], F32, name="sq_sum")
             squares = norm.tile([P, D], BF16)
             nc.scalar.activation(
                 out=squares[:],
@@ -231,18 +231,23 @@ def tile_bertselfattention_pb_t_kernel(tc, probs, x, Wv, gamma, beta, out):
                 func=ACT.Square,
                 bias=neg_mean_of[m][:],
                 scale=1.0,
-                accum_out=sq_sum[:],
+                accum_out=sq_sum_of[n][:, r : r + 1],
             )
-            nc.gpsimd.tensor_scalar(
-                out=var_eps[:],
-                in0=sq_sum[:],
-                scalar1=1.0 / D,
-                scalar2=LN_EPS,
-                op0=ALU.mult,
-                op1=ALU.add,
-            )
-            nc.gpsimd.tensor_tensor(out=rstd[:], in0=var_eps[:], in1=minus_half[:], op=ALU.pow)
-            rstd_of[m] = rstd
+            if r == ROW_PAIR - 1:
+                var_eps = norm.tile([P, ROW_PAIR], F32)
+                rstd = norm.tile([P, ROW_PAIR], F32)
+                nc.gpsimd.tensor_scalar(
+                    out=var_eps[:],
+                    in0=sq_sum_of[n][:],
+                    scalar1=1.0 / D,
+                    scalar2=LN_EPS,
+                    op0=ALU.mult,
+                    op1=ALU.add,
+                )
+                nc.gpsimd.tensor_tensor(
+                    out=rstd[:], in0=var_eps[:], in1=minus_half[:], op=ALU.pow
+                )
+                rstd_of[n] = rstd
 
         def finish(m):
             n, r = divmod(m, ROW_PAIR)
@@ -252,7 +257,7 @@ def tile_bertselfattention_pb_t_kernel(tc, probs, x, Wv, gamma, beta, out):
             nc.vector.scalar_tensor_tensor(
                 out=result_of[n][:, r, :],
                 in0=scaled_of[m][:],
-                scalar=rstd_of[m][:],
+                scalar=rstd_of[n][:, r : r + 1],
                 in1=gain_bias[:, 1, :],
                 op0=ALU.mult,
                 op1=ALU.add,
@@ -265,7 +270,7 @@ def tile_bertselfattention_pb_t_kernel(tc, probs, x, Wv, gamma, beta, out):
 
         ident = consts.tile([P, P], F32)
         make_identity(nc, ident[:])
-        minus_half = consts.tile([P, 1], F32)
+        minus_half = consts.tile([P, ROW_PAIR], F32)
         nc.vector.memset(minus_half[:], -0.5)
         ones = consts.tile([P, P], BF16)
         nc.vector.memset(ones[:], 1.0)

@@ -234,18 +234,13 @@ def tile_bertselfattention_pb_t_kernel(tc, probs, x, Wv, gamma, beta, out):
                 accum_out=sq_sum_of[n][:, r : r + 1],
             )
             if r == ROW_PAIR - 1:
-                var_eps = norm.tile([P, ROW_PAIR], F32)
                 rstd = norm.tile([P, ROW_PAIR], F32)
-                nc.gpsimd.tensor_scalar(
-                    out=var_eps[:],
-                    in0=sq_sum_of[n][:],
-                    scalar1=1.0 / D,
-                    scalar2=LN_EPS,
-                    op0=ALU.mult,
-                    op1=ALU.add,
-                )
-                nc.gpsimd.tensor_tensor(
-                    out=rstd[:], in0=var_eps[:], in1=minus_half[:], op=ALU.pow
+                nc.scalar.activation(
+                    out=rstd[:],
+                    in_=sq_sum_of[n][:],
+                    func=ACT.Abs_reciprocal_sqrt,
+                    bias=LN_EPS,
+                    scale=1.0 / D,
                 )
                 rstd_of[n] = rstd
 
@@ -270,8 +265,6 @@ def tile_bertselfattention_pb_t_kernel(tc, probs, x, Wv, gamma, beta, out):
 
         ident = consts.tile([P, P], F32)
         make_identity(nc, ident[:])
-        minus_half = consts.tile([P, ROW_PAIR], F32)
-        nc.vector.memset(minus_half[:], -0.5)
         ones = consts.tile([P, P], BF16)
         nc.vector.memset(ones[:], 1.0)
         gb_row = consts.tile([P, 2, D], BF16)

@@ -29,8 +29,8 @@ HALVES = D // P
 COLS = H * P
 AHEAD = 6
 X_STEPS = PASSES + 1
-LAG = {"T": 0, "Q": 1, "M": 2, "K": 3, "Y": 3, "R": 4, "N": 4, "H": 5, "D": 4, "F": 7}
-ORDER = "TRQMKYFNHD"
+LAG = {"T": 0, "Q": 1, "M": 2, "C": 2, "K": 3, "Y": 3, "R": 4, "N": 4, "H": 5, "D": 4, "S": 5, "F": 7}
+ORDER = "TRQMCKYFNHDS"
 X_LOAD = {1: 1, 2: 4, 3: 7}
 X_AT = {1: (2, 3, 4), 2: (7, 10, 13), 3: (16, 19, 22)}
 W_AT = 1
@@ -50,7 +50,7 @@ def tile_bertselfattention_pb_t_kernel(tc, probs, x, Wv, gamma, beta, out):
         stack.enter_context(tc.manual_schedule())
 
         rows_of, x_rows_of, x_grouped_of, x_codes_of, x_scales_of = {}, {}, {}, {}, {}
-        grouped_of, codes_of, scales_of = {}, {}, {}
+        grouped_of, codes_of, scales_of, ctx_of = {}, {}, {}, {}
         merged_of, m_codes_of, m_scales_of, y_of = {}, {}, {}, {}
         yres_of, row_sum_of, neg_mean_of, rstd_of, scaled_of, result_of, sq_sum_of = {}, {}, {}, {}, {}, {}, {}
 
@@ -159,6 +159,10 @@ def tile_bertselfattention_pb_t_kernel(tc, probs, x, Wv, gamma, beta, out):
                         start=(g == 0),
                         stop=(g == PASSES - 1),
                     )
+            ctx_of[m] = ctx_t
+
+        def copy_ctx(m):
+            ctx_t = ctx_of[m]
             merged = work.tile([P, P, PACK], BF16, align_bytes=64)
             nc.scalar.copy(out=merged[:], in_=ctx_t[:].rearrange("p t c -> p c t"))
             merged_of[m] = merged
@@ -233,6 +237,9 @@ def tile_bertselfattention_pb_t_kernel(tc, probs, x, Wv, gamma, beta, out):
                 scale=1.0,
                 accum_out=sq_sum_of[n][:, r : r + 1],
             )
+
+        def spread(m):
+            n, r = divmod(m, ROW_PAIR)
             if r == ROW_PAIR - 1:
                 rstd = norm.tile([P, ROW_PAIR], F32)
                 nc.scalar.activation(
@@ -324,12 +331,14 @@ def tile_bertselfattention_pb_t_kernel(tc, probs, x, Wv, gamma, beta, out):
             "T": turn_unit,
             "Q": quantise_unit,
             "M": pool_values,
+            "C": copy_ctx,
             "K": quantise_merged,
             "Y": project,
             "R": add_residual,
             "N": negate_mean,
             "H": centre_and_gain,
             "D": deviation,
+            "S": spread,
             "F": finish,
         }
         for it in range(UNITS + max(LAG.values())):

@@ -29,8 +29,8 @@ HALVES = D // P
 COLS = H * P
 AHEAD = 6
 X_STEPS = PASSES + 1
-LAG = {"T": 0, "Q": 1, "M": 2, "C": 2, "K": 3, "Y": 3, "R": 4, "N": 4, "H": 5, "D": 4, "S": 5, "F": 7}
-ORDER = "TRQMCKYFNHDS"
+LAG = {"T": 0, "E": 0, "Q": 1, "M": 2, "C": 2, "K": 3, "Y": 4, "R": 5, "N": 5, "H": 6, "D": 6, "S": 7, "F": 9}
+ORDER = "TERQMCYFKNHDS"
 X_LOAD = {1: 1, 2: 4, 3: 7}
 X_AT = {1: (2, 3, 4), 2: (7, 10, 13), 3: (16, 19, 22)}
 W_AT = 1
@@ -42,15 +42,15 @@ def tile_bertselfattention_pb_t_kernel(tc, probs, x, Wv, gamma, beta, out):
         consts = stack.enter_context(tc.tile_pool(name="consts", bufs=1))
         rows_pool = stack.enter_context(tc.tile_pool(name="rows", bufs=AHEAD + 1))
         x_pool = stack.enter_context(tc.tile_pool(name="x", bufs=2))
-        work = stack.enter_context(tc.tile_pool(name="work", bufs=4))
-        norm = stack.enter_context(tc.tile_pool(name="norm", bufs=4))
+        work = stack.enter_context(tc.tile_pool(name="work", bufs=5))
+        norm = stack.enter_context(tc.tile_pool(name="norm", bufs=6))
         turn_banks = stack.enter_context(tc.psum_pool(name="turn_banks", bufs=4))
         ctx_banks = stack.enter_context(tc.psum_pool(name="ctx_banks", bufs=2))
         y_banks = stack.enter_context(tc.psum_pool(name="y_banks", bufs=2))
         stack.enter_context(tc.manual_schedule())
 
         rows_of, x_rows_of, x_grouped_of, x_codes_of, x_scales_of = {}, {}, {}, {}, {}
-        grouped_of, codes_of, scales_of, ctx_of = {}, {}, {}, {}
+        turned_of, grouped_of, codes_of, scales_of, ctx_of = {}, {}, {}, {}, {}
         merged_of, m_codes_of, m_scales_of, y_of = {}, {}, {}, {}
         yres_of, row_sum_of, neg_mean_of, rstd_of, scaled_of, result_of, sq_sum_of = {}, {}, {}, {}, {}, {}, {}
 
@@ -116,11 +116,7 @@ def tile_bertselfattention_pb_t_kernel(tc, probs, x, Wv, gamma, beta, out):
 
         def turn_unit(m):
             n, r = divmod(m, ROW_PAIR)
-            grouped = work.tile([P, PASSES * COLS * PACK], BF16, align_bytes=64)
-            grouped_of[m] = grouped
-            grouped_words = grouped[:].bitcast(F32).rearrange(
-                "p (g h c u) -> p g h c u", g=PASSES, h=H, u=TURNS
-            )
+            turned_of[m] = []
             for h in range(H):
                 words = rows_of[n][:, h, r, :].bitcast(F32)
                 turned = turn_banks.tile([P, PASSES, TURNS, P], F32)
@@ -130,9 +126,18 @@ def tile_bertselfattention_pb_t_kernel(tc, probs, x, Wv, gamma, beta, out):
                         nc.tensor.transpose(
                             turned[:, g, u, :], words[:, first : first + P], ident[:]
                         )
+                turned_of[m].append(turned)
+
+        def copy_turned(m):
+            grouped = work.tile([P, PASSES * COLS * PACK], BF16, align_bytes=64)
+            grouped_of[m] = grouped
+            grouped_words = grouped[:].bitcast(F32).rearrange(
+                "p (g h c u) -> p g h c u", g=PASSES, h=H, u=TURNS
+            )
+            for h in range(H):
                 nc.scalar.copy(
                     out=grouped_words[:, :, h, :, :],
-                    in_=turned[:].rearrange("p g u c -> p g c u"),
+                    in_=turned_of[m][h][:].rearrange("p g u c -> p g c u"),
                 )
 
         def quantise_unit(m):
@@ -329,6 +334,7 @@ def tile_bertselfattention_pb_t_kernel(tc, probs, x, Wv, gamma, beta, out):
 
         stages = {
             "T": turn_unit,
+            "E": copy_turned,
             "Q": quantise_unit,
             "M": pool_values,
             "C": copy_ctx,

@@ -29,8 +29,9 @@ HALVES = D // P
 COLS = H * P
 AHEAD = 6
 X_STEPS = PASSES + 1
-LAG = {"T": 0, "E": 0, "Q": 1, "M": 2, "C": 2, "K": 3, "Y": 4, "R": 5, "N": 5, "H": 6, "D": 6, "S": 7, "F": 9}
-ORDER = "TERQMCYFKNHDS"
+LAG = {"T": 0, "E": 0, "Q": 1, "M": 2, "C": 2, "K": 3, "Y": 4, "R": 5, "N": 5, "H": 6, "D": 5, "S": 6, "F": 8}
+ORDER = "TERHFQMSYNKCD"
+V_COPY = (23, 27)
 X_LOAD = {1: 1, 2: 4, 3: 7}
 X_AT = {1: (2, 3, 4), 2: (7, 10, 13), 3: (16, 19, 22)}
 W_AT = 1
@@ -169,7 +170,8 @@ def tile_bertselfattention_pb_t_kernel(tc, probs, x, Wv, gamma, beta, out):
         def copy_ctx(m):
             ctx_t = ctx_of[m]
             merged = work.tile([P, P, PACK], BF16, align_bytes=64)
-            nc.scalar.copy(out=merged[:], in_=ctx_t[:].rearrange("p t c -> p c t"))
+            copy_out = nc.vector.tensor_copy if m in V_COPY else nc.scalar.copy
+            copy_out(out=merged[:], in_=ctx_t[:].rearrange("p t c -> p c t"))
             merged_of[m] = merged
 
         def quantise_merged(m):
@@ -277,6 +279,16 @@ def tile_bertselfattention_pb_t_kernel(tc, probs, x, Wv, gamma, beta, out):
 
         ident = consts.tile([P, P], F32)
         make_identity(nc, ident[:])
+        one = consts.tile([P, 1], F32)
+        nc.vector.memset(one[:], 1.0)
+        table_probe = consts.tile([P, 1], F32)
+        nc.scalar.activation(
+            out=table_probe[:],
+            in_=one[:],
+            func=ACT.Abs_reciprocal_sqrt,
+            bias=LN_EPS,
+            scale=1.0 / D,
+        )
         ones = consts.tile([P, P], BF16)
         nc.vector.memset(ones[:], 1.0)
         gb_row = consts.tile([P, 2, D], BF16)
@@ -320,6 +332,7 @@ def tile_bertselfattention_pb_t_kernel(tc, probs, x, Wv, gamma, beta, out):
         load_x(0)
         load_unit(0, 1)
         load_weights()
+
         def load_slab_and_x(n):
             load_slab(n)
             for b in range(1, B):

@@ -29,9 +29,9 @@ HALVES = D // P
 COLS = H * P
 AHEAD = 6
 X_STEPS = PASSES + 1
-LAG = {"T": 0, "E": 0, "Q": 1, "M": 2, "C": 2, "K": 3, "Y": 4, "R": 5, "N": 5, "H": 6, "D": 5, "S": 6, "F": 8}
+LAG = {"T": 0, "E": 0, "Q": 1, "M": 2, "C": 2, "K": 3, "Y": 4, "R": 5, "N": 5, "H": 7, "D": 5, "S": 6, "F": 8}
 ORDER = "TERHFQMSYNKCD"
-V_COPY = (23, 27)
+V_COPY = (15, 21, 27)
 X_LOAD = {1: 1, 2: 4, 3: 7}
 X_AT = {1: (2, 3, 4), 2: (7, 10, 13), 3: (16, 19, 22)}
 W_AT = 1
@@ -199,8 +199,10 @@ def tile_bertselfattention_pb_t_kernel(tc, probs, x, Wv, gamma, beta, out):
 
         def add_residual(m):
             b, q = divmod(m, SLABS * ROW_PAIR)
+            n, r = divmod(m, ROW_PAIR)
+            if r == 0:
+                row_sum_of[n] = norm.tile([P, ROW_PAIR], F32, name="row_sum")
             yres = norm.tile([P, D], F32)
-            row_sum = norm.tile([P, 1], F32)
             nc.vector.scalar_tensor_tensor(
                 out=yres[:],
                 in0=y_of[m][:, :D],
@@ -208,23 +210,35 @@ def tile_bertselfattention_pb_t_kernel(tc, probs, x, Wv, gamma, beta, out):
                 in1=x_rows_of[b][:, q, :],
                 op0=ALU.mult,
                 op1=ALU.add,
-                accum_out=row_sum[:],
+                accum_out=row_sum_of[n][:, r : r + 1],
             )
-            yres_of[m], row_sum_of[m] = yres, row_sum
+            yres_of[m] = yres
 
         def negate_mean(m):
-            neg_mean = norm.tile([P, 1], F32)
+            n, r = divmod(m, ROW_PAIR)
+            if r == 0:
+                neg_mean_of[n] = norm.tile([P, ROW_PAIR], F32, name="neg_mean")
+            if n == N_SLABS - 1:
+                cols = slice(r, r + 1)
+            elif r == ROW_PAIR - 1:
+                cols = slice(0, ROW_PAIR)
+            else:
+                return
             nc.vector.tensor_scalar(
-                out=neg_mean[:], in0=row_sum_of[m][:], scalar1=-1.0 / D, scalar2=None, op0=ALU.mult
+                out=neg_mean_of[n][:, cols],
+                in0=row_sum_of[n][:, cols],
+                scalar1=-1.0 / D,
+                scalar2=None,
+                op0=ALU.mult,
             )
-            neg_mean_of[m] = neg_mean
 
         def centre_and_gain(m):
+            n, r = divmod(m, ROW_PAIR)
             scaled = norm.tile([P, D], F32)
             nc.vector.scalar_tensor_tensor(
                 out=scaled[:],
                 in0=yres_of[m][:],
-                scalar=neg_mean_of[m][:],
+                scalar=neg_mean_of[n][:, r : r + 1],
                 in1=gain_bias[:, 0, :],
                 op0=ALU.add,
                 op1=ALU.mult,
@@ -240,8 +254,8 @@ def tile_bertselfattention_pb_t_kernel(tc, probs, x, Wv, gamma, beta, out):
                 out=squares[:],
                 in_=yres_of[m][:],
                 func=ACT.Square,
-                bias=neg_mean_of[m][:],
-                scale=1.0,
+                bias=row_sum_of[n][:, r : r + 1],
+                scale=-float(D),
                 accum_out=sq_sum_of[n][:, r : r + 1],
             )
 
@@ -254,7 +268,7 @@ def tile_bertselfattention_pb_t_kernel(tc, probs, x, Wv, gamma, beta, out):
                     in_=sq_sum_of[n][:],
                     func=ACT.Abs_reciprocal_sqrt,
                     bias=LN_EPS,
-                    scale=1.0 / D,
+                    scale=1.0 / D**3,
                 )
                 rstd_of[n] = rstd
 

@@ -30,11 +30,11 @@ COLS = H * P
 AHEAD = 6
 X_STEPS = PASSES + 1
 LAG = {"T": 0, "E": 0, "Q": 1, "M": 2, "C": 2, "K": 3, "Y": 4, "R": 5, "N": 5, "H": 7, "D": 5, "S": 6, "F": 8}
-ORDER = "TERHFQMSYNKCD"
-V_COPY = (15, 21, 27)
-X_LOAD = {1: 1, 2: 4, 3: 7}
-X_AT = {1: (2, 3, 4), 2: (7, 10, 13), 3: (16, 19, 22)}
-W_AT = 1
+ORDER = "TERHMQSFYNKCD"
+V_COPY = range(5, UNITS - 1, 9)
+X_LOAD = {1: 2, 2: 4, 3: 6}
+X_AT = {1: (4, 5, 6), 2: (9, 12, 15), 3: (17, 20, 23)}
+W_AT = 3
 
 
 def tile_bertselfattention_pb_t_kernel(tc, probs, x, Wv, gamma, beta, out):
@@ -345,7 +345,6 @@ def tile_bertselfattention_pb_t_kernel(tc, probs, x, Wv, gamma, beta, out):
         load_unit(0, 0)
         load_x(0)
         load_unit(0, 1)
-        load_weights()
 
         def load_slab_and_x(n):
             load_slab(n)
@@ -355,6 +354,8 @@ def tile_bertselfattention_pb_t_kernel(tc, probs, x, Wv, gamma, beta, out):
 
         for n in range(1, AHEAD):
             load_slab_and_x(n)
+            if n == 1:
+                load_weights()
 
         def live(m):
             return 0 <= m < UNITS

from contextlib import ExitStack

import concourse.mybir as mybir
from concourse.masks import make_identity

F32 = mybir.dt.float32
BF16 = mybir.dt.bfloat16
U32 = mybir.dt.uint32
U8 = mybir.dt.uint8
FP8X4 = mybir.dt.float8_e4m3fn_x4
ALU = mybir.AluOpType
ACT = mybir.ActivationFunctionType

B, H, S, D = 4, 2, 1024, 256
LN_EPS = 1e-5
FLOPS = 2 * B * H * S * S * D + 2 * B * S * (H * D) * D

P = 128
BANK = 512
PACK = 4
PASSES = S // (P * PACK)
TURNS = 2
ROW_PAIR = 2
SLAB = P * ROW_PAIR
SLABS = S // SLAB
N_SLABS = B * SLABS
UNITS = N_SLABS * ROW_PAIR
HALVES = D // P
COLS = H * P
AHEAD = 6
X_STEPS = PASSES + 1
LAG = {"T": 0, "E": 0, "Q": 1, "M": 2, "C": 2, "K": 3, "Y": 4, "R": 5, "N": 5, "H": 7, "D": 5, "S": 6, "F": 8}
ORDER = "TERHMQSFYNKCD"
V_COPY = range(5, UNITS - 1, 9)
X_LOAD = {1: 2, 2: 4, 3: 6}
X_AT = {1: (4, 5, 6), 2: (9, 12, 15), 3: (17, 20, 23)}
W_AT = 3


def tile_bertselfattention_pb_t_kernel(tc, probs, x, Wv, gamma, beta, out):
    nc = tc.nc
    with ExitStack() as stack:
        consts = stack.enter_context(tc.tile_pool(name="consts", bufs=1))
        rows_pool = stack.enter_context(tc.tile_pool(name="rows", bufs=AHEAD + 1))
        x_pool = stack.enter_context(tc.tile_pool(name="x", bufs=2))
        work = stack.enter_context(tc.tile_pool(name="work", bufs=5))
        norm = stack.enter_context(tc.tile_pool(name="norm", bufs=6))
        turn_banks = stack.enter_context(tc.psum_pool(name="turn_banks", bufs=4))
        ctx_banks = stack.enter_context(tc.psum_pool(name="ctx_banks", bufs=2))
        y_banks = stack.enter_context(tc.psum_pool(name="y_banks", bufs=2))
        stack.enter_context(tc.manual_schedule())

        rows_of, x_rows_of, x_grouped_of, x_codes_of, x_scales_of = {}, {}, {}, {}, {}
        turned_of, grouped_of, codes_of, scales_of, ctx_of = {}, {}, {}, {}, {}
        merged_of, m_codes_of, m_scales_of, y_of = {}, {}, {}, {}
        yres_of, row_sum_of, neg_mean_of, rstd_of, scaled_of, result_of, sq_sum_of = {}, {}, {}, {}, {}, {}, {}

        def probs_rows(n, h):
            b, a = divmod(n, SLABS)
            return probs[b, h, a * SLAB : (a + 1) * SLAB, :]

        def new_rows(n):
            rows_of[n] = rows_pool.tile([P, H, ROW_PAIR, S], BF16, name="rows")

        def load_unit(n, r):
            for h in range(H):
                nc.sync.dma_start(
                    out=rows_of[n][:, h, r, :],
                    in_=probs_rows(n, h).rearrange("(p r) j -> r p j", r=ROW_PAIR)[r],
                )

        def load_slab(n):
            new_rows(n)
            for h in range(H):
                nc.sync.dma_start(
                    out=rows_of[n][:, h, :, :].rearrange("p r j -> p (r j)"),
                    in_=probs_rows(n, h).rearrange("(p r) j -> p (r j)", r=ROW_PAIR),
                )

        def load_x(b):
            x_rows = x_pool.tile([P, SLABS * ROW_PAIR, D], BF16, bufs=B)
            nc.sync.dma_start(
                out=x_rows[:].rearrange("p (a r) d -> p a (r d)", r=ROW_PAIR),
                in_=x[b].rearrange("(a p r) d -> p a (r d)", p=P, r=ROW_PAIR),
            )
            x_rows_of[b] = x_rows

        def regroup(grouped, planes):
            nc.vector.tensor_copy(
                out=grouped.rearrange("p (c i) t -> p c t i", i=4),
                in_=planes.rearrange("p t (c i) -> p c t i", i=4),
            )

        def regroup_x(b, g):
            if g == 0:
                x_grouped_of[b] = x_pool.tile(
                    [P, PASSES, D, PACK], BF16, align_bytes=64, name="x_grouped"
                )
            regroup(x_grouped_of[b][:, g, :, :], x_rows_of[b][:, g * PACK : (g + 1) * PACK, :])

        def quantise_x(b):
            x_codes = x_pool.tile([P, PASSES * D], U32, align_bytes=64, bufs=B)
            x_scales = x_pool.tile([P, PASSES * D], U8, align_bytes=64, bufs=B)
            nc.vector.quantize_mx(
                out=x_codes[:].bitcast(FP8X4),
                scales=x_scales[:],
                in_=x_grouped_of[b][:].rearrange("p g d t -> p (g d t)"),
            )
            x_codes_of[b], x_scales_of[b] = x_codes, x_scales

        def prepare_x(b, steps):
            for step in steps:
                if step < PASSES:
                    regroup_x(b, step)
                else:
                    quantise_x(b)

        def turn_unit(m):
            n, r = divmod(m, ROW_PAIR)
            turned_of[m] = []
            for h in range(H):
                words = rows_of[n][:, h, r, :].bitcast(F32)
                turned = turn_banks.tile([P, PASSES, TURNS, P], F32)
                for g in range(PASSES):
                    for u in range(TURNS):
                        first = (g * TURNS + u) * P
                        nc.tensor.transpose(
                            turned[:, g, u, :], words[:, first : first + P], ident[:]
                        )
                turned_of[m].append(turned)

        def copy_turned(m):
            grouped = work.tile([P, PASSES * COLS * PACK], BF16, align_bytes=64)
            grouped_of[m] = grouped
            grouped_words = grouped[:].bitcast(F32).rearrange(
                "p (g h c u) -> p g h c u", g=PASSES, h=H, u=TURNS
            )
            for h in range(H):
                nc.scalar.copy(
                    out=grouped_words[:, :, h, :, :],
                    in_=turned_of[m][h][:].rearrange("p g u c -> p g c u"),
                )

        def quantise_unit(m):
            codes = work.tile([P, PASSES * COLS], U32, align_bytes=64)
            scales = work.tile([P, PASSES * COLS], U8, align_bytes=64)
            nc.vector.quantize_mx(
                out=codes[:].bitcast(FP8X4), scales=scales[:], in_=grouped_of[m][:]
            )
            codes_of[m], scales_of[m] = codes, scales

        def pool_values(m):
            b = m // (SLABS * ROW_PAIR)
            ctx_t = ctx_banks.tile([P, PACK, P], F32)
            for f in range(HALVES):
                for g in range(PASSES):
                    x_cols = slice(g * D + f * P, g * D + (f + 1) * P)
                    q_cols = slice(g * COLS, (g + 1) * COLS)
                    nc.tensor.matmul_mx(
                        out=ctx_t[:, f * H : (f + 1) * H, :].rearrange("p h c -> p (h c)"),
                        lhsT=x_codes_of[b][:, x_cols].bitcast(FP8X4),
                        lhsT_scale=x_scales_of[b][:, x_cols],
                        rhs=codes_of[m][:, q_cols].bitcast(FP8X4),
                        rhs_scale=scales_of[m][:, q_cols],
                        start=(g == 0),
                        stop=(g == PASSES - 1),
                    )
            ctx_of[m] = ctx_t

        def copy_ctx(m):
            ctx_t = ctx_of[m]
            merged = work.tile([P, P, PACK], BF16, align_bytes=64)
            copy_out = nc.vector.tensor_copy if m in V_COPY else nc.scalar.copy
            copy_out(out=merged[:], in_=ctx_t[:].rearrange("p t c -> p c t"))
            merged_of[m] = merged

        def quantise_merged(m):
            m_codes = work.tile([P, P], U32, align_bytes=64)
            m_scales = work.tile([P, P], U8, align_bytes=64)
            nc.vector.quantize_mx(
                out=m_codes[:].bitcast(FP8X4),
                scales=m_scales[:],
                in_=merged_of[m][:].rearrange("p c t -> p (c t)"),
            )
            m_codes_of[m], m_scales_of[m] = m_codes, m_scales

        def project(m):
            y = y_banks.tile([P, BANK], F32)
            nc.tensor.matmul_mx(
                out=y[:, :D],
                lhsT=m_codes_of[m][:].bitcast(FP8X4),
                lhsT_scale=m_scales_of[m][:],
                rhs=w_codes[:].bitcast(FP8X4),
                rhs_scale=w_scales[:],
                start=True,
                stop=True,
            )
            y_of[m] = y

        def add_residual(m):
            b, q = divmod(m, SLABS * ROW_PAIR)
            n, r = divmod(m, ROW_PAIR)
            if r == 0:
                row_sum_of[n] = norm.tile([P, ROW_PAIR], F32, name="row_sum")
            yres = norm.tile([P, D], F32)
            nc.vector.scalar_tensor_tensor(
                out=yres[:],
                in0=y_of[m][:, :D],
                scalar=1.0,
                in1=x_rows_of[b][:, q, :],
                op0=ALU.mult,
                op1=ALU.add,
                accum_out=row_sum_of[n][:, r : r + 1],
            )
            yres_of[m] = yres

        def negate_mean(m):
            n, r = divmod(m, ROW_PAIR)
            if r == 0:
                neg_mean_of[n] = norm.tile([P, ROW_PAIR], F32, name="neg_mean")
            if n == N_SLABS - 1:
                cols = slice(r, r + 1)
            elif r == ROW_PAIR - 1:
                cols = slice(0, ROW_PAIR)
            else:
                return
            nc.vector.tensor_scalar(
                out=neg_mean_of[n][:, cols],
                in0=row_sum_of[n][:, cols],
                scalar1=-1.0 / D,
                scalar2=None,
                op0=ALU.mult,
            )

        def centre_and_gain(m):
            n, r = divmod(m, ROW_PAIR)
            scaled = norm.tile([P, D], F32)
            nc.vector.scalar_tensor_tensor(
                out=scaled[:],
                in0=yres_of[m][:],
                scalar=neg_mean_of[n][:, r : r + 1],
                in1=gain_bias[:, 0, :],
                op0=ALU.add,
                op1=ALU.mult,
            )
            scaled_of[m] = scaled

        def deviation(m):
            n, r = divmod(m, ROW_PAIR)
            if r == 0:
                sq_sum_of[n] = norm.tile([P, ROW_PAIR], F32, name="sq_sum")
            squares = norm.tile([P, D], BF16)
            nc.scalar.activation(
                out=squares[:],
                in_=yres_of[m][:],
                func=ACT.Square,
                bias=row_sum_of[n][:, r : r + 1],
                scale=-float(D),
                accum_out=sq_sum_of[n][:, r : r + 1],
            )

        def spread(m):
            n, r = divmod(m, ROW_PAIR)
            if r == ROW_PAIR - 1:
                rstd = norm.tile([P, ROW_PAIR], F32)
                nc.scalar.activation(
                    out=rstd[:],
                    in_=sq_sum_of[n][:],
                    func=ACT.Abs_reciprocal_sqrt,
                    bias=LN_EPS,
                    scale=1.0 / D**3,
                )
                rstd_of[n] = rstd

        def finish(m):
            n, r = divmod(m, ROW_PAIR)
            b, a = divmod(n, SLABS)
            if r == 0:
                result_of[n] = norm.tile([P, ROW_PAIR, D], F32, name="result")
            nc.vector.scalar_tensor_tensor(
                out=result_of[n][:, r, :],
                in0=scaled_of[m][:],
                scalar=rstd_of[n][:, r : r + 1],
                in1=gain_bias[:, 1, :],
                op0=ALU.mult,
                op1=ALU.add,
            )
            rows = out[b, a * SLAB : (a + 1) * SLAB, :].rearrange("(p r) e -> p r e", r=ROW_PAIR)
            if n == N_SLABS - 1:
                nc.sync.dma_start(out=rows[:, r, :], in_=result_of[n][:, r, :])
            elif r == ROW_PAIR - 1:
                nc.sync.dma_start(out=rows, in_=result_of[n][:])

        ident = consts.tile([P, P], F32)
        make_identity(nc, ident[:])
        one = consts.tile([P, 1], F32)
        nc.vector.memset(one[:], 1.0)
        table_probe = consts.tile([P, 1], F32)
        nc.scalar.activation(
            out=table_probe[:],
            in_=one[:],
            func=ACT.Abs_reciprocal_sqrt,
            bias=LN_EPS,
            scale=1.0 / D,
        )
        ones = consts.tile([P, P], BF16)
        nc.vector.memset(ones[:], 1.0)
        gb_row = consts.tile([P, 2, D], BF16)
        nc.vector.memset(gb_row[:], 0.0)
        gain_bias = consts.tile([P, 2, D], F32)
        w_rows = consts.tile([P, PACK, D], BF16)
        w_grouped = consts.tile([P, D, PACK], BF16, align_bytes=64)
        w_codes = consts.tile([P, D], U32, align_bytes=64)
        w_scales = consts.tile([P, D], U8, align_bytes=64)

        def load_weights():
            for f in range(HALVES):
                nc.sync.dma_start(
                    out=w_rows[:, f * H : (f + 1) * H, :],
                    in_=Wv.rearrange("(h f p) e -> f p h e", h=H, f=HALVES)[f],
                )
            nc.sync.dma_start(out=gb_row[0:1, 0, :], in_=gamma.rearrange("(o e) -> o e", o=1))
            nc.sync.dma_start(out=gb_row[0:1, 1, :], in_=beta.rearrange("(o e) -> o e", o=1))

        def prepare_weights():
            regroup(w_grouped[:], w_rows[:])
            nc.vector.quantize_mx(
                out=w_codes[:].bitcast(FP8X4),
                scales=w_scales[:],
                in_=w_grouped[:].rearrange("p e t -> p (e t)"),
            )

        def spread_gain_bias():
            gb_bank = y_banks.tile([P, BANK], F32, tag="y")
            nc.tensor.matmul(
                out=gb_bank[:],
                lhsT=ones[:],
                rhs=gb_row[:].rearrange("p k e -> p (k e)"),
                start=True,
                stop=True,
            )
            nc.scalar.copy(out=gain_bias[:].rearrange("p k e -> p (k e)"), in_=gb_bank[:])

        new_rows(0)
        load_unit(0, 0)
        load_x(0)
        load_unit(0, 1)

        def load_slab_and_x(n):
            load_slab(n)
            for b in range(1, B):
                if X_LOAD[b] == n:
                    load_x(b)

        for n in range(1, AHEAD):
            load_slab_and_x(n)
            if n == 1:
                load_weights()

        def live(m):
            return 0 <= m < UNITS

        stages = {
            "T": turn_unit,
            "E": copy_turned,
            "Q": quantise_unit,
            "M": pool_values,
            "C": copy_ctx,
            "K": quantise_merged,
            "Y": project,
            "R": add_residual,
            "N": negate_mean,
            "H": centre_and_gain,
            "D": deviation,
            "S": spread,
            "F": finish,
        }
        for it in range(UNITS + max(LAG.values())):
            if it % ROW_PAIR == 0 and it // ROW_PAIR + AHEAD < N_SLABS:
                load_slab_and_x(it // ROW_PAIR + AHEAD)
            for key in ORDER:
                if live(it - LAG[key]):
                    stages[key](it - LAG[key])
                if key == "T" and it == 0:
                    prepare_x(0, range(X_STEPS))
            if it == W_AT:
                prepare_weights()
                spread_gain_bias()
            for b in range(1, B):
                if it in X_AT[b]:
                    prepare_x(b, [X_AT[b].index(it)])
